import numpy as np
import ml_dtypes

BF16 = ml_dtypes.bfloat16


def bf(x):
    return np.asarray(x, np.float32).astype(BF16)


def f32(x):
    return np.asarray(x, np.float32)


def f64(x):
    return np.asarray(x).astype(np.float64)


def striped(idx):
    return np.tile(idx.reshape(-1, 16).T, (8, 1))


C, S, N, K, R = 128, 2048, 1024, 16, 640
EPS_STD = 1e-5
EPS_GN = 1e-5


def setup_inputs():
    base = f32(np.random.standard_normal((C, S)))
    x = f32(np.random.standard_normal((C, N)))
    loc = 0.5 * np.random.standard_normal((C, N, 1))
    spread = 0.5 + np.random.random((C, N, 1))
    m = f32(loc + spread * np.random.standard_normal((C, N, K)))
    w_post = bf(np.random.standard_normal((R, C)) / np.sqrt(R))
    w_lin = bf(np.random.standard_normal((C, C)) / np.sqrt(C))
    gn_w = f32(1.0 + 0.1 * np.random.standard_normal((C, 1)))
    gn_b = f32(0.1 * np.random.standard_normal((C, 1)))
    gn_alpha = f32(1.0 + 0.1 * np.random.standard_normal((C, 1)))
    return {"base": base, "x": x, "m": m, "w_post": w_post, "w_lin": w_lin, "gn_w": gn_w, "gn_b": gn_b, "gn_alpha": gn_alpha, "offs": striped(np.random.permutation(S)[:N])}


def reference(base, x, m, w_post, w_lin, gn_w, gn_b, gn_alpha, offs):
    idx = offs[:16].T.reshape(-1)
    x = f64(x)
    m = f64(m)
    mean = m.mean(axis=2)
    mn = m.min(axis=2)
    mx = m.max(axis=2)
    var = (m * m).mean(axis=2) - mean * mean
    std = np.sqrt(np.maximum(var, 0.0) + EPS_STD)
    cat = np.concatenate([x, mean, mn, mx, std], axis=0)
    h = f64(w_post).T @ cat
    u = f64(w_lin).T @ h
    mu = u.mean(axis=1, keepdims=True)
    z = u - f64(gn_alpha) * mu
    v = (z * z).mean(axis=1, keepdims=True)
    y = np.maximum(f64(gn_w) * z / np.sqrt(v + EPS_GN) + f64(gn_b), 0.0)
    out = f64(base).copy()
    out[:, idx] = y + x
    return out

@@ -1,0 +1,111 @@
+import concourse.mybir as mybir
+
+F32 = mybir.dt.float32
+BF16 = mybir.dt.bfloat16
+U16 = mybir.dt.uint16
+ALU = mybir.AluOpType
+ACT = mybir.ActivationFunctionType
+X_AXIS = mybir.AxisListType.X
+
+P = 128
+STORE = 2048
+NODES = 1024
+MSGS = 16
+BLOCKS = 5
+CHUNK = 128
+N_CHUNKS = NODES // CHUNK
+BANK = 512
+EPS = 1e-5
+
+FLOPS = 2 * BLOCKS * P * P * NODES + 2 * P * P * NODES
+
+
+def tile_gnnlayer_kernel(tc, base, x, m, w_post, w_lin, gn_w, gn_b, gn_alpha, offs, out):
+    nc = tc.nc
+    with (
+        tc.tile_pool(name="held", bufs=1) as held,
+        tc.tile_pool(name="msgs", bufs=3) as msgs,
+        tc.tile_pool(name="work", bufs=3) as work,
+        tc.psum_pool(name="psum_h", bufs=2) as psum_h,
+        tc.psum_pool(name="psum_u", bufs=1) as psum_u,
+    ):
+        offsets = held.tile([P, NODES // 16], U16, name="offsets")
+        nc.sync.dma_start(offsets[:], offs)
+        store = held.tile([P, STORE], F32, name="store")
+        nc.scalar.dma_start(store[:], base)
+        x_f32 = held.tile([P, NODES], F32, name="x_f32")
+        nc.scalar.dma_start(x_f32[:], x)
+        w_post_sb = held.tile([P, BLOCKS, P], BF16, name="w_post_sb")
+        nc.scalar.dma_start(w_post_sb[:], w_post.rearrange("(b r) d -> r b d", r=P))
+        w_lin_sb = held.tile([P, P], BF16, name="w_lin_sb")
+        nc.scalar.dma_start(w_lin_sb[:], w_lin)
+        weight = held.tile([P, 1], F32, name="weight")
+        nc.scalar.dma_start(weight[:], gn_w)
+        shift = held.tile([P, 1], F32, name="shift")
+        nc.scalar.dma_start(shift[:], gn_b)
+        alpha = held.tile([P, 1], F32, name="alpha")
+        nc.scalar.dma_start(alpha[:], gn_alpha)
+
+        cat = held.tile([P, BLOCKS, NODES], BF16, name="cat")
+        nc.gpsimd.tensor_copy(cat[:, 0, :], x_f32[:])
+
+        u_banks = [psum_u.tile([P, BANK], F32, name=f"u_bank{k}") for k in range(NODES // BANK)]
+        u_stats = held.tile([P, N_CHUNKS, 6], F32, name="u_stats")
+
+        for i in range(N_CHUNKS):
+            nodes = slice(i * CHUNK, (i + 1) * CHUNK)
+            msg = msgs.tile([P, CHUNK, MSGS], F32, name="msg")
+            nc.sync.dma_start(msg[:], m[:, nodes, :])
+
+            squares = msgs.tile([P, CHUNK, MSGS], F32, name="squares")
+            nc.scalar.activation(squares[:], msg[:], ACT.Square)
+            total = work.tile([P, CHUNK], F32, name="total")
+            nc.vector.tensor_reduce(total[:], msg[:], X_AXIS, ALU.add)
+            total_sq = work.tile([P, CHUNK], F32, name="total_sq")
+            nc.vector.tensor_reduce(total_sq[:], squares[:], X_AXIS, ALU.add)
+            with nc.allow_low_precision(reason="min and max pick an element; only the result is rounded"):
+                nc.vector.tensor_reduce(cat[:, 2, nodes], msg[:], X_AXIS, ALU.min)
+                nc.vector.tensor_reduce(cat[:, 3, nodes], msg[:], X_AXIS, ALU.max)
+
+            nc.scalar.activation(cat[:, 1, nodes], total[:], ACT.Copy, scale=1.0 / MSGS)
+            mean_sq = work.tile([P, CHUNK], F32, name="mean_sq")
+            nc.scalar.activation(mean_sq[:], total[:], ACT.Square, scale=1.0 / MSGS)
+            var = work.tile([P, CHUNK], F32, name="var")
+            nc.vector.scalar_tensor_tensor(var[:], total_sq[:], 1.0 / MSGS, mean_sq[:], ALU.mult, ALU.subtract)
+            nc.vector.tensor_scalar(var[:], var[:], 0.0, EPS, ALU.max, ALU.add)
+            nc.scalar.activation(cat[:, 4, nodes], var[:], ACT.Sqrt)
+
+            h_ps = psum_h.tile([P, CHUNK], F32, name="h_ps")
+            for b in range(BLOCKS):
+                nc.tensor.matmul(h_ps[:], w_post_sb[:, b, :], cat[:, b, nodes], start=(b == 0), stop=(b == BLOCKS - 1))
+            h_bf = work.tile([P, CHUNK], BF16, name="h_bf")
+            nc.scalar.copy(h_bf[:], h_ps[:])
+            u_chunk = u_banks[i * CHUNK // BANK][:, (i * CHUNK) % BANK : (i * CHUNK) % BANK + CHUNK]
+            nc.tensor.matmul(u_chunk, w_lin_sb[:], h_bf[:], start=True, stop=True)
+            nc.vector.bn_stats(u_stats[:, i, :], u_chunk)
+
+        mean_var = held.tile([P, 2], F32, name="mean_var")
+        nc.vector.bn_aggr(mean_var[:], u_stats[:].rearrange("p c s -> p (c s)"))
+        mu = mean_var[:, 0:1]
+        var_u = mean_var[:, 1:2]
+        alpha_mu = held.tile([P, 1], F32, name="alpha_mu")
+        nc.vector.tensor_mul(alpha_mu[:], alpha[:], mu)
+        z_mean = held.tile([P, 1], F32, name="z_mean")
+        nc.vector.tensor_sub(z_mean[:], mu, alpha_mu[:])
+        v_eps = held.tile([P, 1], F32, name="v_eps")
+        nc.vector.scalar_tensor_tensor(v_eps[:], z_mean[:], z_mean[:], var_u, ALU.mult, ALU.add)
+        nc.vector.tensor_scalar_add(v_eps[:], v_eps[:], EPS)
+        norm = held.tile([P, 1], F32, name="norm")
+        nc.scalar.activation(norm[:], v_eps[:], ACT.Sqrt)
+        gain = held.tile([P, 1], F32, name="gain")
+        nc.vector.reciprocal(gain[:], norm[:])
+        nc.vector.tensor_mul(gain[:], gain[:], weight[:])
+        offset = held.tile([P, 1], F32, name="offset")
+        nc.vector.tensor_mul(offset[:], gain[:], alpha_mu[:])
+        nc.vector.tensor_sub(offset[:], shift[:], offset[:])
+        y = held.tile([P, NODES], F32, name="y")
+        for k, u_bank in enumerate(u_banks):
+            nc.scalar.activation(y[:, k * BANK : (k + 1) * BANK], u_bank[:], ACT.Relu, bias=offset[:], scale=gain[:])
+
+        nc.vector.tensor_tensor(store[:].indirect(offsets[:]), y[:], x_f32[:], ALU.add)
+        nc.sync.dma_start(out, store[:])

@@ -26,6 +26,7 @@ def tile_gnnlayer_kernel(tc, base, x, m, w_post, w_lin, gn_w, gn_b, gn_alpha, of
         tc.tile_pool(name="held", bufs=1) as held,
         tc.tile_pool(name="msgs", bufs=3) as msgs,
         tc.tile_pool(name="work", bufs=3) as work,
+        tc.tile_pool(name="folds", bufs=2) as folds,
         tc.psum_pool(name="psum_h", bufs=2) as psum_h,
         tc.psum_pool(name="psum_u", bufs=1) as psum_u,
     ):
@@ -63,9 +64,17 @@ def tile_gnnlayer_kernel(tc, base, x, m, w_post, w_lin, gn_w, gn_b, gn_alpha, of
             nc.vector.tensor_reduce(total[:], msg[:], X_AXIS, ALU.add)
             total_sq = work.tile([P, CHUNK], F32, name="total_sq")
             nc.vector.tensor_reduce(total_sq[:], squares[:], X_AXIS, ALU.add)
-            with nc.allow_low_precision(reason="min and max pick an element; only the result is rounded"):
-                nc.vector.tensor_reduce(cat[:, 2, nodes], msg[:], X_AXIS, ALU.min)
-                nc.vector.tensor_reduce(cat[:, 3, nodes], msg[:], X_AXIS, ALU.max)
+            msg_bf = msgs.tile([P, CHUNK, MSGS], BF16, name="msg_bf")
+            nc.scalar.copy(msg_bf[:], msg[:])
+            for block, op, label in ((2, ALU.min, "min"), (3, ALU.max, "max")):
+                folded = msg_bf
+                width = MSGS // 2
+                while width > 1:
+                    halved = folds.tile([P, CHUNK, width], BF16, name=f"{label}{width}")
+                    nc.vector.tensor_tensor(halved[:], folded[:, :, 0:width], folded[:, :, width : 2 * width], op)
+                    folded = halved
+                    width //= 2
+                nc.vector.tensor_tensor(cat[:, block, nodes], folded[:, :, 0], folded[:, :, 1], op)
 
             nc.scalar.activation(cat[:, 1, nodes], total[:], ACT.Copy, scale=1.0 / MSGS)
             mean_sq = work.tile([P, CHUNK], F32, name="mean_sq")

@@ -1,4 +1,5 @@
 import concourse.mybir as mybir
+from concourse.masks import make_identity
 
 F32 = mybir.dt.float32
 BF16 = mybir.dt.bfloat16
@@ -28,6 +29,7 @@ def tile_gnnlayer_kernel(tc, base, x, m, w_post, w_lin, gn_w, gn_b, gn_alpha, of
         tc.tile_pool(name="work", bufs=3) as work,
         tc.tile_pool(name="folds", bufs=2) as folds,
         tc.psum_pool(name="psum_h", bufs=2) as psum_h,
+        tc.psum_pool(name="psum_sq", bufs=2) as psum_sq,
         tc.psum_pool(name="psum_u", bufs=1) as psum_u,
     ):
         offsets = held.tile([P, NODES // 16], U16, name="offsets")
@@ -47,6 +49,9 @@ def tile_gnnlayer_kernel(tc, base, x, m, w_post, w_lin, gn_w, gn_b, gn_alpha, of
         alpha = held.tile([P, 1], F32, name="alpha")
         nc.scalar.dma_start(alpha[:], gn_alpha)
 
+        identity = held.tile([P, P], F32, name="identity")
+        make_identity(nc, identity[:])
+
         cat = held.tile([P, BLOCKS, NODES], BF16, name="cat")
         nc.gpsimd.tensor_copy(cat[:, 0, :], x_f32[:])
 
@@ -62,8 +67,9 @@ def tile_gnnlayer_kernel(tc, base, x, m, w_post, w_lin, gn_w, gn_b, gn_alpha, of
             nc.scalar.activation(squares[:], msg[:], ACT.Square)
             total = work.tile([P, CHUNK], F32, name="total")
             nc.vector.tensor_reduce(total[:], msg[:], X_AXIS, ALU.add)
-            total_sq = work.tile([P, CHUNK], F32, name="total_sq")
-            nc.vector.tensor_reduce(total_sq[:], squares[:], X_AXIS, ALU.add)
+            total_sq = psum_sq.tile([P, CHUNK], F32, name="total_sq")
+            for t in range(MSGS):
+                nc.tensor.matmul(total_sq[:], identity[:], squares[:, :, t], start=(t == 0), stop=(t == MSGS - 1))
             msg_bf = msgs.tile([P, CHUNK, MSGS], BF16, name="msg_bf")
             nc.scalar.copy(msg_bf[:], msg[:])
             for block, op, label in ((2, ALU.min, "min"), (3, ALU.max, "max")):

@@ -15,6 +15,7 @@ MSGS = 16
 BLOCKS = 5
 CHUNK = 128
 N_CHUNKS = NODES // CHUNK
+LINE = 4
 BANK = 512
 EPS = 1e-5
 
@@ -25,29 +26,34 @@ def tile_gnnlayer_kernel(tc, base, x, m, w_post, w_lin, gn_w, gn_b, gn_alpha, of
     nc = tc.nc
     with (
         tc.tile_pool(name="held", bufs=1) as held,
-        tc.tile_pool(name="msgs", bufs=3) as msgs,
-        tc.tile_pool(name="work", bufs=3) as work,
+        tc.tile_pool(name="msgs", bufs=N_CHUNKS) as msgs,
+        tc.tile_pool(name="copies", bufs=3) as copies,
         tc.tile_pool(name="folds", bufs=2) as folds,
-        tc.psum_pool(name="psum_h", bufs=2) as psum_h,
+        tc.tile_pool(name="work", bufs=3) as work,
         tc.psum_pool(name="psum_sq", bufs=2) as psum_sq,
+        tc.psum_pool(name="psum_h", bufs=2) as psum_h,
         tc.psum_pool(name="psum_u", bufs=1) as psum_u,
     ):
         offsets = held.tile([P, NODES // 16], U16, name="offsets")
         nc.sync.dma_start(offsets[:], offs)
-        store = held.tile([P, STORE], F32, name="store")
-        nc.scalar.dma_start(store[:], base)
-        x_f32 = held.tile([P, NODES], F32, name="x_f32")
-        nc.scalar.dma_start(x_f32[:], x)
+        msg_tiles = [msgs.tile([P, CHUNK, MSGS], F32, name="msg") for i in range(N_CHUNKS)]
+        nc.sync.dma_start(msg_tiles[0][:], m[:, 0:CHUNK, :])
         w_post_sb = held.tile([P, BLOCKS, P], BF16, name="w_post_sb")
-        nc.scalar.dma_start(w_post_sb[:], w_post.rearrange("(b r) d -> r b d", r=P))
+        nc.sync.dma_start(w_post_sb[:], w_post.rearrange("(b r) d -> r b d", r=P))
         w_lin_sb = held.tile([P, P], BF16, name="w_lin_sb")
-        nc.scalar.dma_start(w_lin_sb[:], w_lin)
+        nc.sync.dma_start(w_lin_sb[:], w_lin)
+        x_f32 = held.tile([P, NODES], F32, name="x_f32")
+        nc.sync.dma_start(x_f32[:], x)
+        for i in range(1, N_CHUNKS):
+            nc.sync.dma_start(msg_tiles[i][:], m[:, i * CHUNK : (i + 1) * CHUNK, :])
         weight = held.tile([P, 1], F32, name="weight")
-        nc.scalar.dma_start(weight[:], gn_w)
+        nc.sync.dma_start(weight[:], gn_w)
         shift = held.tile([P, 1], F32, name="shift")
-        nc.scalar.dma_start(shift[:], gn_b)
+        nc.sync.dma_start(shift[:], gn_b)
         alpha = held.tile([P, 1], F32, name="alpha")
-        nc.scalar.dma_start(alpha[:], gn_alpha)
+        nc.sync.dma_start(alpha[:], gn_alpha)
+        store = held.tile([P, STORE], F32, name="store")
+        nc.sync.dma_start(store[:], base)
 
         identity = held.tile([P, P], F32, name="identity")
         make_identity(nc, identity[:])
@@ -58,19 +64,23 @@ def tile_gnnlayer_kernel(tc, base, x, m, w_post, w_lin, gn_w, gn_b, gn_alpha, of
         u_banks = [psum_u.tile([P, BANK], F32, name=f"u_bank{k}") for k in range(NODES // BANK)]
         u_stats = held.tile([P, N_CHUNKS, 6], F32, name="u_stats")
 
-        for i in range(N_CHUNKS):
+        def aggregate(i):
             nodes = slice(i * CHUNK, (i + 1) * CHUNK)
-            msg = msgs.tile([P, CHUNK, MSGS], F32, name="msg")
-            nc.sync.dma_start(msg[:], m[:, nodes, :])
+            msg = msg_tiles[i]
 
-            squares = msgs.tile([P, CHUNK, MSGS], F32, name="squares")
-            nc.scalar.activation(squares[:], msg[:], ACT.Square)
+            squares = copies.tile([P, MSGS, CHUNK], F32, name="squares")
+            total_sq = psum_sq.tile([P, CHUNK], F32, name="total_sq")
+            for t0 in range(0, MSGS, LINE):
+                nc.scalar.activation(
+                    squares[:, t0 : t0 + LINE, :].rearrange("p t j -> p j t"), msg[:, :, t0 : t0 + LINE], ACT.Square
+                )
+                for t in range(t0, t0 + LINE):
+                    nc.tensor.matmul(total_sq[:], identity[:], squares[:, t, :], start=(t == 0), stop=(t == MSGS - 1))
+
             total = work.tile([P, CHUNK], F32, name="total")
             nc.vector.tensor_reduce(total[:], msg[:], X_AXIS, ALU.add)
-            total_sq = psum_sq.tile([P, CHUNK], F32, name="total_sq")
-            for t in range(MSGS):
-                nc.tensor.matmul(total_sq[:], identity[:], squares[:, :, t], start=(t == 0), stop=(t == MSGS - 1))
-            msg_bf = msgs.tile([P, CHUNK, MSGS], BF16, name="msg_bf")
+
+            msg_bf = copies.tile([P, CHUNK, MSGS], BF16, name="msg_bf")
             nc.scalar.copy(msg_bf[:], msg[:])
             for block, op, label in ((2, ALU.min, "min"), (3, ALU.max, "max")):
                 folded = msg_bf
@@ -81,7 +91,10 @@ def tile_gnnlayer_kernel(tc, base, x, m, w_post, w_lin, gn_w, gn_b, gn_alpha, of
                     folded = halved
                     width //= 2
                 nc.vector.tensor_tensor(cat[:, block, nodes], folded[:, :, 0], folded[:, :, 1], op)
+            return total, total_sq
 
+        def finish(i, total, total_sq):
+            nodes = slice(i * CHUNK, (i + 1) * CHUNK)
             nc.scalar.activation(cat[:, 1, nodes], total[:], ACT.Copy, scale=1.0 / MSGS)
             mean_sq = work.tile([P, CHUNK], F32, name="mean_sq")
             nc.scalar.activation(mean_sq[:], total[:], ACT.Square, scale=1.0 / MSGS)
@@ -98,6 +111,13 @@ def tile_gnnlayer_kernel(tc, base, x, m, w_post, w_lin, gn_w, gn_b, gn_alpha, of
             u_chunk = u_banks[i * CHUNK // BANK][:, (i * CHUNK) % BANK : (i * CHUNK) % BANK + CHUNK]
             nc.tensor.matmul(u_chunk, w_lin_sb[:], h_bf[:], start=True, stop=True)
             nc.vector.bn_stats(u_stats[:, i, :], u_chunk)
+
+        sums = aggregate(0)
+        for i in range(1, N_CHUNKS):
+            earlier = sums
+            sums = aggregate(i)
+            finish(i - 1, earlier[0], earlier[1])
+        finish(N_CHUNKS - 1, sums[0], sums[1])
 
         mean_var = held.tile([P, 2], F32, name="mean_var")
         nc.vector.bn_aggr(mean_var[:], u_stats[:].rearrange("p c s -> p (c s)"))

@@ -15,7 +15,6 @@ MSGS = 16
 BLOCKS = 5
 CHUNK = 128
 N_CHUNKS = NODES // CHUNK
-LINE = 4
 BANK = 512
 EPS = 1e-5
 
@@ -30,7 +29,8 @@ def tile_gnnlayer_kernel(tc, base, x, m, w_post, w_lin, gn_w, gn_b, gn_alpha, of
         tc.tile_pool(name="copies", bufs=3) as copies,
         tc.tile_pool(name="folds", bufs=2) as folds,
         tc.tile_pool(name="work", bufs=3) as work,
-        tc.psum_pool(name="psum_sq", bufs=2) as psum_sq,
+        tc.psum_pool(name="psum_flipped", bufs=2) as psum_flipped,
+        tc.psum_pool(name="psum_sums", bufs=2) as psum_sums,
         tc.psum_pool(name="psum_h", bufs=2) as psum_h,
         tc.psum_pool(name="psum_u", bufs=1) as psum_u,
     ):
@@ -61,6 +61,12 @@ def tile_gnnlayer_kernel(tc, base, x, m, w_post, w_lin, gn_w, gn_b, gn_alpha, of
         cat = held.tile([P, BLOCKS, NODES], BF16, name="cat")
         nc.gpsimd.tensor_copy(cat[:, 0, :], x_f32[:])
 
+        one_minus_alpha = held.tile([P, 1], F32, name="one_minus_alpha")
+        nc.gpsimd.tensor_scalar(one_minus_alpha[:], alpha[:], -1.0, 1.0, ALU.mult, ALU.add)
+        minus_w_alpha = held.tile([P, 1], F32, name="minus_w_alpha")
+        nc.gpsimd.tensor_tensor(minus_w_alpha[:], weight[:], alpha[:], ALU.mult)
+        nc.gpsimd.tensor_scalar_mul(minus_w_alpha[:], minus_w_alpha[:], -1.0)
+
         u_banks = [psum_u.tile([P, BANK], F32, name=f"u_bank{k}") for k in range(NODES // BANK)]
         u_stats = held.tile([P, N_CHUNKS, 6], F32, name="u_stats")
 
@@ -68,22 +74,23 @@ def tile_gnnlayer_kernel(tc, base, x, m, w_post, w_lin, gn_w, gn_b, gn_alpha, of
             nodes = slice(i * CHUNK, (i + 1) * CHUNK)
             msg = msg_tiles[i]
 
-            squares = copies.tile([P, MSGS, CHUNK], F32, name="squares")
-            total_sq = psum_sq.tile([P, CHUNK], F32, name="total_sq")
-            for t0 in range(0, MSGS, LINE):
-                nc.scalar.activation(
-                    squares[:, t0 : t0 + LINE, :].rearrange("p t j -> p j t"), msg[:, :, t0 : t0 + LINE], ACT.Square
-                )
-                for t in range(t0, t0 + LINE):
-                    nc.tensor.matmul(total_sq[:], identity[:], squares[:, t, :], start=(t == 0), stop=(t == MSGS - 1))
+            squares = copies.tile([P, CHUNK, MSGS], F32, name="squares")
+            nc.scalar.activation(squares[:], msg[:], ACT.Square)
 
-            total = work.tile([P, CHUNK], F32, name="total")
-            nc.vector.tensor_reduce(total[:], msg[:], X_AXIS, ALU.add)
+            flipped = psum_flipped.tile([P, 2, P], F32, name="flipped")
+            for k, values in enumerate((msg, squares)):
+                for t in range(MSGS):
+                    nc.tensor.matmul(
+                        flipped[:, k, :], values[:, :, t], identity[:], start=(t == 0), stop=(t == MSGS - 1), is_transpose=True
+                    )
+            flipped_sb = work.tile([P, 2, P], F32, name="flipped_sb")
+            nc.scalar.copy(flipped_sb[:], flipped[:])
+            sums = psum_sums.tile([P, 2, CHUNK], F32, name="sums")
+            for k in range(2):
+                nc.tensor.transpose(sums[:, k, :], flipped_sb[:, k, :], identity[:])
 
-            msg_bf = copies.tile([P, CHUNK, MSGS], BF16, name="msg_bf")
-            nc.scalar.copy(msg_bf[:], msg[:])
             for block, op, label in ((2, ALU.min, "min"), (3, ALU.max, "max")):
-                folded = msg_bf
+                folded = msg
                 width = MSGS // 2
                 while width > 1:
                     halved = folds.tile([P, CHUNK, width], BF16, name=f"{label}{width}")
@@ -91,15 +98,15 @@ def tile_gnnlayer_kernel(tc, base, x, m, w_post, w_lin, gn_w, gn_b, gn_alpha, of
                     folded = halved
                     width //= 2
                 nc.vector.tensor_tensor(cat[:, block, nodes], folded[:, :, 0], folded[:, :, 1], op)
-            return total, total_sq
+            return sums[:, 0, :], sums[:, 1, :]
 
         def finish(i, total, total_sq):
             nodes = slice(i * CHUNK, (i + 1) * CHUNK)
-            nc.scalar.activation(cat[:, 1, nodes], total[:], ACT.Copy, scale=1.0 / MSGS)
+            nc.scalar.activation(cat[:, 1, nodes], total, ACT.Copy, scale=1.0 / MSGS)
             mean_sq = work.tile([P, CHUNK], F32, name="mean_sq")
-            nc.scalar.activation(mean_sq[:], total[:], ACT.Square, scale=1.0 / MSGS)
+            nc.scalar.activation(mean_sq[:], total, ACT.Square, scale=1.0 / MSGS)
             var = work.tile([P, CHUNK], F32, name="var")
-            nc.vector.scalar_tensor_tensor(var[:], total_sq[:], 1.0 / MSGS, mean_sq[:], ALU.mult, ALU.subtract)
+            nc.vector.scalar_tensor_tensor(var[:], total_sq, 1.0 / MSGS, mean_sq[:], ALU.mult, ALU.subtract)
             nc.vector.tensor_scalar(var[:], var[:], 0.0, EPS, ALU.max, ALU.add)
             nc.scalar.activation(cat[:, 4, nodes], var[:], ACT.Sqrt)
 
@@ -123,21 +130,20 @@ def tile_gnnlayer_kernel(tc, base, x, m, w_post, w_lin, gn_w, gn_b, gn_alpha, of
         nc.vector.bn_aggr(mean_var[:], u_stats[:].rearrange("p c s -> p (c s)"))
         mu = mean_var[:, 0:1]
         var_u = mean_var[:, 1:2]
-        alpha_mu = held.tile([P, 1], F32, name="alpha_mu")
-        nc.vector.tensor_mul(alpha_mu[:], alpha[:], mu)
-        z_mean = held.tile([P, 1], F32, name="z_mean")
-        nc.vector.tensor_sub(z_mean[:], mu, alpha_mu[:])
-        v_eps = held.tile([P, 1], F32, name="v_eps")
-        nc.vector.scalar_tensor_tensor(v_eps[:], z_mean[:], z_mean[:], var_u, ALU.mult, ALU.add)
-        nc.vector.tensor_scalar_add(v_eps[:], v_eps[:], EPS)
+        z_mean_sq = held.tile([P, 1], F32, name="z_mean_sq")
+        nc.scalar.activation(z_mean_sq[:], mu, ACT.Square, scale=one_minus_alpha[:])
+        var_eps = held.tile([P, 1], F32, name="var_eps")
+        nc.vector.tensor_scalar_add(var_eps[:], var_u, EPS)
+        minus_w_alpha_mu = held.tile([P, 1], F32, name="minus_w_alpha_mu")
+        nc.vector.tensor_mul(minus_w_alpha_mu[:], minus_w_alpha[:], mu)
         norm = held.tile([P, 1], F32, name="norm")
-        nc.scalar.activation(norm[:], v_eps[:], ACT.Sqrt)
+        nc.scalar.activation(norm[:], z_mean_sq[:], ACT.Sqrt, bias=var_eps[:])
+        inv_norm = held.tile([P, 1], F32, name="inv_norm")
+        nc.vector.reciprocal(inv_norm[:], norm[:])
         gain = held.tile([P, 1], F32, name="gain")
-        nc.vector.reciprocal(gain[:], norm[:])
-        nc.vector.tensor_mul(gain[:], gain[:], weight[:])
+        nc.vector.tensor_mul(gain[:], weight[:], inv_norm[:])
         offset = held.tile([P, 1], F32, name="offset")
-        nc.vector.tensor_mul(offset[:], gain[:], alpha_mu[:])
-        nc.vector.tensor_sub(offset[:], shift[:], offset[:])
+        nc.vector.tensor_scalar(offset[:], inv_norm[:], minus_w_alpha_mu[:], shift[:], ALU.mult, ALU.add)
         y = held.tile([P, NODES], F32, name="y")
         for k, u_bank in enumerate(u_banks):
             nc.scalar.activation(y[:, k * BANK : (k + 1) * BANK], u_bank[:], ACT.Relu, bias=offset[:], scale=gain[:])

@@ -26,9 +26,9 @@ def tile_gnnlayer_kernel(tc, base, x, m, w_post, w_lin, gn_w, gn_b, gn_alpha, of
     with (
         tc.tile_pool(name="held", bufs=1) as held,
         tc.tile_pool(name="msgs", bufs=N_CHUNKS) as msgs,
-        tc.tile_pool(name="copies", bufs=3) as copies,
-        tc.tile_pool(name="folds", bufs=2) as folds,
-        tc.tile_pool(name="work", bufs=3) as work,
+        tc.tile_pool(name="copies", bufs=4) as copies,
+        tc.tile_pool(name="folds", bufs=3) as folds,
+        tc.tile_pool(name="work", bufs=4) as work,
         tc.psum_pool(name="psum_flipped", bufs=2) as psum_flipped,
         tc.psum_pool(name="psum_sums", bufs=2) as psum_sums,
         tc.psum_pool(name="psum_h", bufs=2) as psum_h,
@@ -73,24 +73,36 @@ def tile_gnnlayer_kernel(tc, base, x, m, w_post, w_lin, gn_w, gn_b, gn_alpha, of
         def aggregate(i):
             nodes = slice(i * CHUNK, (i + 1) * CHUNK)
             msg = msg_tiles[i]
+            tensor_sums_messages = i % 2 == 0
 
             squares = copies.tile([P, CHUNK, MSGS], F32, name="squares")
             nc.scalar.activation(squares[:], msg[:], ACT.Square)
 
+            summed = (msg, squares) if tensor_sums_messages else (squares,)
             flipped = psum_flipped.tile([P, 2, P], F32, name="flipped")
-            for k, values in enumerate((msg, squares)):
+            for k, values in enumerate(summed):
                 for t in range(MSGS):
                     nc.tensor.matmul(
                         flipped[:, k, :], values[:, :, t], identity[:], start=(t == 0), stop=(t == MSGS - 1), is_transpose=True
                     )
             flipped_sb = work.tile([P, 2, P], F32, name="flipped_sb")
-            nc.scalar.copy(flipped_sb[:], flipped[:])
+            nc.scalar.copy(flipped_sb[:, 0 : len(summed), :], flipped[:, 0 : len(summed), :])
             sums = psum_sums.tile([P, 2, CHUNK], F32, name="sums")
-            for k in range(2):
+            for k in range(len(summed)):
                 nc.tensor.transpose(sums[:, k, :], flipped_sb[:, k, :], identity[:])
+            total_sq = sums[:, len(summed) - 1, :]
 
+            if tensor_sums_messages:
+                total = sums[:, 0, :]
+                folded_first = msg
+            else:
+                total_sb = work.tile([P, CHUNK], F32, name="total_sb")
+                nc.vector.tensor_reduce(total_sb[:], msg[:], X_AXIS, ALU.add)
+                total = total_sb[:]
+                folded_first = copies.tile([P, CHUNK, MSGS], BF16, name="msg_bf")
+                nc.scalar.copy(folded_first[:], msg[:])
             for block, op, label in ((2, ALU.min, "min"), (3, ALU.max, "max")):
-                folded = msg
+                folded = folded_first
                 width = MSGS // 2
                 while width > 1:
                     halved = folds.tile([P, CHUNK, width], BF16, name=f"{label}{width}")
@@ -98,7 +110,7 @@ def tile_gnnlayer_kernel(tc, base, x, m, w_post, w_lin, gn_w, gn_b, gn_alpha, of
                     folded = halved
                     width //= 2
                 nc.vector.tensor_tensor(cat[:, block, nodes], folded[:, :, 0], folded[:, :, 1], op)
-            return sums[:, 0, :], sums[:, 1, :]
+            return total, total_sq
 
         def finish(i, total, total_sq):
             nodes = slice(i * CHUNK, (i + 1) * CHUNK)

@@ -13,9 +13,12 @@ STORE = 2048
 NODES = 1024
 MSGS = 16
 BLOCKS = 5
-CHUNK = 128
+HALF = 128
+CHUNK = 2 * HALF
 N_CHUNKS = NODES // CHUNK
+N_SUMS = 3
 BANK = 512
+BN_STATS = 6
 EPS = 1e-5
 
 FLOPS = 2 * BLOCKS * P * P * NODES + 2 * P * P * NODES
@@ -26,9 +29,9 @@ def tile_gnnlayer_kernel(tc, base, x, m, w_post, w_lin, gn_w, gn_b, gn_alpha, of
     with (
         tc.tile_pool(name="held", bufs=1) as held,
         tc.tile_pool(name="msgs", bufs=N_CHUNKS) as msgs,
-        tc.tile_pool(name="copies", bufs=4) as copies,
-        tc.tile_pool(name="folds", bufs=3) as folds,
-        tc.tile_pool(name="work", bufs=4) as work,
+        tc.tile_pool(name="copies", bufs=2) as copies,
+        tc.tile_pool(name="folds", bufs=2) as folds,
+        tc.tile_pool(name="work", bufs=3) as work,
         tc.psum_pool(name="psum_flipped", bufs=2) as psum_flipped,
         tc.psum_pool(name="psum_sums", bufs=2) as psum_sums,
         tc.psum_pool(name="psum_h", bufs=2) as psum_h,
@@ -37,7 +40,14 @@ def tile_gnnlayer_kernel(tc, base, x, m, w_post, w_lin, gn_w, gn_b, gn_alpha, of
         offsets = held.tile([P, NODES // 16], U16, name="offsets")
         nc.sync.dma_start(offsets[:], offs)
         msg_tiles = [msgs.tile([P, CHUNK, MSGS], F32, name="msg") for i in range(N_CHUNKS)]
-        nc.sync.dma_start(msg_tiles[0][:], m[:, 0:CHUNK, :])
+
+        def load_messages(i):
+            for first in (0, HALF):
+                nc.sync.dma_start(
+                    msg_tiles[i][:, first : first + HALF, :], m[:, i * CHUNK + first : i * CHUNK + first + HALF, :]
+                )
+
+        load_messages(0)
         w_post_sb = held.tile([P, BLOCKS, P], BF16, name="w_post_sb")
         nc.sync.dma_start(w_post_sb[:], w_post.rearrange("(b r) d -> r b d", r=P))
         w_lin_sb = held.tile([P, P], BF16, name="w_lin_sb")
@@ -45,7 +55,7 @@ def tile_gnnlayer_kernel(tc, base, x, m, w_post, w_lin, gn_w, gn_b, gn_alpha, of
         x_f32 = held.tile([P, NODES], F32, name="x_f32")
         nc.sync.dma_start(x_f32[:], x)
         for i in range(1, N_CHUNKS):
-            nc.sync.dma_start(msg_tiles[i][:], m[:, i * CHUNK : (i + 1) * CHUNK, :])
+            load_messages(i)
         weight = held.tile([P, 1], F32, name="weight")
         nc.sync.dma_start(weight[:], gn_w)
         shift = held.tile([P, 1], F32, name="shift")
@@ -68,55 +78,60 @@ def tile_gnnlayer_kernel(tc, base, x, m, w_post, w_lin, gn_w, gn_b, gn_alpha, of
         nc.gpsimd.tensor_scalar_mul(minus_w_alpha[:], minus_w_alpha[:], -1.0)
 
         u_banks = [psum_u.tile([P, BANK], F32, name=f"u_bank{k}") for k in range(NODES // BANK)]
-        u_stats = held.tile([P, N_CHUNKS, 6], F32, name="u_stats")
+        u_stats = held.tile([P, N_CHUNKS, BN_STATS], F32, name="u_stats")
+
+        def sum_flipped(flipped_sum, values):
+            for t in range(MSGS):
+                nc.tensor.matmul(
+                    flipped_sum, values[:, :, t], identity[:], start=(t == 0), stop=(t == MSGS - 1), is_transpose=True
+                )
 
         def aggregate(i):
             nodes = slice(i * CHUNK, (i + 1) * CHUNK)
-            msg = msg_tiles[i]
-            tensor_sums_messages = i % 2 == 0
+            first_half = msg_tiles[i][:, 0:HALF, :]
+            second_half = msg_tiles[i][:, HALF:CHUNK, :]
 
+            flipped = psum_flipped.tile([P, N_SUMS, HALF], F32, name="flipped")
             squares = copies.tile([P, CHUNK, MSGS], F32, name="squares")
-            nc.scalar.activation(squares[:], msg[:], ACT.Square)
+            sum_flipped(flipped[:, 0, :], first_half)
+            nc.scalar.activation(squares[:, 0:HALF, :], first_half, ACT.Square)
+            sum_flipped(flipped[:, 1, :], squares[:, 0:HALF, :])
+            nc.scalar.activation(squares[:, HALF:CHUNK, :], second_half, ACT.Square)
+            sum_flipped(flipped[:, 2, :], squares[:, HALF:CHUNK, :])
 
-            summed = (msg, squares) if tensor_sums_messages else (squares,)
-            flipped = psum_flipped.tile([P, 2, P], F32, name="flipped")
-            for k, values in enumerate(summed):
-                for t in range(MSGS):
-                    nc.tensor.matmul(
-                        flipped[:, k, :], values[:, :, t], identity[:], start=(t == 0), stop=(t == MSGS - 1), is_transpose=True
-                    )
-            flipped_sb = work.tile([P, 2, P], F32, name="flipped_sb")
-            nc.scalar.copy(flipped_sb[:, 0 : len(summed), :], flipped[:, 0 : len(summed), :])
-            sums = psum_sums.tile([P, 2, CHUNK], F32, name="sums")
-            for k in range(len(summed)):
-                nc.tensor.transpose(sums[:, k, :], flipped_sb[:, k, :], identity[:])
-            total_sq = sums[:, len(summed) - 1, :]
+            second_total = work.tile([P, HALF], F32, name="second_total")
+            nc.vector.tensor_reduce(second_total[:], second_half, X_AXIS, ALU.add)
+            second_bf = copies.tile([P, HALF, MSGS], BF16, name="second_bf")
+            nc.scalar.copy(second_bf[:], second_half)
 
-            if tensor_sums_messages:
-                total = sums[:, 0, :]
-                folded_first = msg
-            else:
-                total_sb = work.tile([P, CHUNK], F32, name="total_sb")
-                nc.vector.tensor_reduce(total_sb[:], msg[:], X_AXIS, ALU.add)
-                total = total_sb[:]
-                folded_first = copies.tile([P, CHUNK, MSGS], BF16, name="msg_bf")
-                nc.scalar.copy(folded_first[:], msg[:])
             for block, op, label in ((2, ALU.min, "min"), (3, ALU.max, "max")):
-                folded = folded_first
                 width = MSGS // 2
-                while width > 1:
+                folded = folds.tile([P, CHUNK, width], BF16, name=f"{label}{width}")
+                nc.vector.tensor_tensor(folded[:, 0:HALF, :], first_half[:, :, 0:width], first_half[:, :, width:MSGS], op)
+                nc.vector.tensor_tensor(folded[:, HALF:CHUNK, :], second_bf[:, :, 0:width], second_bf[:, :, width:MSGS], op)
+                while width > 2:
+                    width //= 2
                     halved = folds.tile([P, CHUNK, width], BF16, name=f"{label}{width}")
                     nc.vector.tensor_tensor(halved[:], folded[:, :, 0:width], folded[:, :, width : 2 * width], op)
                     folded = halved
-                    width //= 2
                 nc.vector.tensor_tensor(cat[:, block, nodes], folded[:, :, 0], folded[:, :, 1], op)
-            return total, total_sq
+            return flipped, second_total
 
-        def finish(i, total, total_sq):
+        def finish(i, flipped, second_total):
             nodes = slice(i * CHUNK, (i + 1) * CHUNK)
-            nc.scalar.activation(cat[:, 1, nodes], total, ACT.Copy, scale=1.0 / MSGS)
+            flipped_sb = work.tile([P, N_SUMS, HALF], F32, name="flipped_sb")
+            nc.scalar.copy(flipped_sb[:], flipped[:])
+            sums = psum_sums.tile([P, N_SUMS, HALF], F32, name="sums")
+            for k in range(N_SUMS):
+                nc.tensor.transpose(sums[:, k, :], flipped_sb[:, k, :], identity[:])
+            total_sq = sums[:, 1:N_SUMS, :].rearrange("p k j -> p (k j)")
+
             mean_sq = work.tile([P, CHUNK], F32, name="mean_sq")
-            nc.scalar.activation(mean_sq[:], total, ACT.Square, scale=1.0 / MSGS)
+            for first, total in ((0, sums[:, 0, :]), (HALF, second_total[:])):
+                nc.scalar.activation(
+                    cat[:, 1, i * CHUNK + first : i * CHUNK + first + HALF], total, ACT.Copy, scale=1.0 / MSGS
+                )
+                nc.scalar.activation(mean_sq[:, first : first + HALF], total, ACT.Square, scale=1.0 / MSGS)
             var = work.tile([P, CHUNK], F32, name="var")
             nc.vector.scalar_tensor_tensor(var[:], total_sq, 1.0 / MSGS, mean_sq[:], ALU.mult, ALU.subtract)
             nc.vector.tensor_scalar(var[:], var[:], 0.0, EPS, ALU.max, ALU.add)
@@ -131,12 +146,12 @@ def tile_gnnlayer_kernel(tc, base, x, m, w_post, w_lin, gn_w, gn_b, gn_alpha, of
             nc.tensor.matmul(u_chunk, w_lin_sb[:], h_bf[:], start=True, stop=True)
             nc.vector.bn_stats(u_stats[:, i, :], u_chunk)
 
-        sums = aggregate(0)
+        partial = aggregate(0)
         for i in range(1, N_CHUNKS):
-            earlier = sums
-            sums = aggregate(i)
+            earlier = partial
+            partial = aggregate(i)
             finish(i - 1, earlier[0], earlier[1])
-        finish(N_CHUNKS - 1, sums[0], sums[1])
+        finish(N_CHUNKS - 1, partial[0], partial[1])
 
         mean_var = held.tile([P, 2], F32, name="mean_var")
         nc.vector.bn_aggr(mean_var[:], u_stats[:].rearrange("p c s -> p (c s)"))

@@ -69,13 +69,12 @@ def tile_gnnlayer_kernel(tc, base, x, m, w_post, w_lin, gn_w, gn_b, gn_alpha, of
         make_identity(nc, identity[:])
 
         cat = held.tile([P, BLOCKS, NODES], BF16, name="cat")
-        nc.gpsimd.tensor_copy(cat[:, 0, :], x_f32[:])
+        nc.vector.tensor_copy(cat[:, 0, :], x_f32[:])
 
         one_minus_alpha = held.tile([P, 1], F32, name="one_minus_alpha")
-        nc.gpsimd.tensor_scalar(one_minus_alpha[:], alpha[:], -1.0, 1.0, ALU.mult, ALU.add)
+        nc.vector.tensor_scalar(one_minus_alpha[:], alpha[:], -1.0, 1.0, ALU.mult, ALU.add)
         minus_w_alpha = held.tile([P, 1], F32, name="minus_w_alpha")
-        nc.gpsimd.tensor_tensor(minus_w_alpha[:], weight[:], alpha[:], ALU.mult)
-        nc.gpsimd.tensor_scalar_mul(minus_w_alpha[:], minus_w_alpha[:], -1.0)
+        nc.vector.scalar_tensor_tensor(minus_w_alpha[:], weight[:], -1.0, alpha[:], ALU.mult, ALU.mult)
 
         u_banks = [psum_u.tile([P, BANK], F32, name=f"u_bank{k}") for k in range(NODES // BANK)]
         u_stats = held.tile([P, N_CHUNKS, BN_STATS], F32, name="u_stats")

@@ -85,24 +85,54 @@ def tile_gnnlayer_kernel(tc, base, x, m, w_post, w_lin, gn_w, gn_b, gn_alpha, of
                     flipped_sum, values[:, :, t], identity[:], start=(t == 0), stop=(t == MSGS - 1), is_transpose=True
                 )
 
-        def aggregate(i):
-            nodes = slice(i * CHUNK, (i + 1) * CHUNK)
-            first_half = msg_tiles[i][:, 0:HALF, :]
-            second_half = msg_tiles[i][:, HALF:CHUNK, :]
+        def tensor_engine_sums_messages(i, k):
+            return k == 0 and i < N_CHUNKS - 1
 
+        def sums(i):
+            halves = (slice(0, HALF), slice(HALF, CHUNK))
             flipped = psum_flipped.tile([P, N_SUMS, HALF], F32, name="flipped")
             squares = copies.tile([P, CHUNK, MSGS], F32, name="squares")
-            sum_flipped(flipped[:, 0, :], first_half)
-            nc.scalar.activation(squares[:, 0:HALF, :], first_half, ACT.Square)
-            sum_flipped(flipped[:, 1, :], squares[:, 0:HALF, :])
-            nc.scalar.activation(squares[:, HALF:CHUNK, :], second_half, ACT.Square)
-            sum_flipped(flipped[:, 2, :], squares[:, HALF:CHUNK, :])
-
-            second_total = work.tile([P, HALF], F32, name="second_total")
-            nc.vector.tensor_reduce(second_total[:], second_half, X_AXIS, ALU.add)
+            vector_totals = work.tile([P, CHUNK], F32, name="vector_totals")
+            for k, half in enumerate(halves):
+                if tensor_engine_sums_messages(i, k):
+                    sum_flipped(flipped[:, 2, :], msg_tiles[i][:, half, :])
+                else:
+                    nc.vector.tensor_reduce(vector_totals[:, half], msg_tiles[i][:, half, :], X_AXIS, ALU.add)
+            for k, half in enumerate(halves):
+                nc.scalar.activation(squares[:, half, :], msg_tiles[i][:, half, :], ACT.Square)
+                sum_flipped(flipped[:, k, :], squares[:, half, :])
             second_bf = copies.tile([P, HALF, MSGS], BF16, name="second_bf")
-            nc.scalar.copy(second_bf[:], second_half)
+            nc.scalar.copy(second_bf[:], msg_tiles[i][:, HALF:CHUNK, :])
+            return flipped, vector_totals, second_bf
 
+        def mean_and_std(i, flipped, vector_totals):
+            nodes = slice(i * CHUNK, (i + 1) * CHUNK)
+            n_flipped = 3 if tensor_engine_sums_messages(i, 0) else 2
+            flipped_sb = work.tile([P, N_SUMS, HALF], F32, name="flipped_sb")
+            nc.scalar.copy(flipped_sb[:, 0:n_flipped, :], flipped[:, 0:n_flipped, :])
+            sums_ps = psum_sums.tile([P, N_SUMS, HALF], F32, name="sums_ps")
+            for k in range(n_flipped):
+                nc.tensor.transpose(sums_ps[:, k, :], flipped_sb[:, k, :], identity[:])
+            total_sq = sums_ps[:, 0:2, :].rearrange("p k j -> p (k j)")
+
+            mean_sq = work.tile([P, CHUNK], F32, name="mean_sq")
+            if tensor_engine_sums_messages(i, 0):
+                pieces = ((slice(0, HALF), sums_ps[:, 2, :]), (slice(HALF, CHUNK), vector_totals[:, HALF:CHUNK]))
+            else:
+                pieces = ((slice(0, CHUNK), vector_totals[:]),)
+            for piece, total in pieces:
+                nc.scalar.activation(
+                    cat[:, 1, i * CHUNK + piece.start : i * CHUNK + piece.stop], total, ACT.Copy, scale=1.0 / MSGS
+                )
+                nc.scalar.activation(mean_sq[:, piece], total, ACT.Square, scale=1.0 / MSGS)
+            var = work.tile([P, CHUNK], F32, name="var")
+            nc.vector.scalar_tensor_tensor(var[:], total_sq, 1.0 / MSGS, mean_sq[:], ALU.mult, ALU.subtract)
+            nc.vector.tensor_scalar(var[:], var[:], 0.0, EPS, ALU.max, ALU.add)
+            nc.scalar.activation(cat[:, 4, nodes], var[:], ACT.Sqrt)
+
+        def min_and_max(i, second_bf):
+            nodes = slice(i * CHUNK, (i + 1) * CHUNK)
+            first_half = msg_tiles[i][:, 0:HALF, :]
             for block, op, label in ((2, ALU.min, "min"), (3, ALU.max, "max")):
                 width = MSGS // 2
                 folded = folds.tile([P, CHUNK, width], BF16, name=f"{label}{width}")
@@ -114,43 +144,27 @@ def tile_gnnlayer_kernel(tc, base, x, m, w_post, w_lin, gn_w, gn_b, gn_alpha, of
                     nc.vector.tensor_tensor(halved[:], folded[:, :, 0:width], folded[:, :, width : 2 * width], op)
                     folded = halved
                 nc.vector.tensor_tensor(cat[:, block, nodes], folded[:, :, 0], folded[:, :, 1], op)
-            return flipped, second_total
 
-        def finish(i, flipped, second_total):
+        def matmuls(i):
             nodes = slice(i * CHUNK, (i + 1) * CHUNK)
-            flipped_sb = work.tile([P, N_SUMS, HALF], F32, name="flipped_sb")
-            nc.scalar.copy(flipped_sb[:], flipped[:])
-            sums = psum_sums.tile([P, N_SUMS, HALF], F32, name="sums")
-            for k in range(N_SUMS):
-                nc.tensor.transpose(sums[:, k, :], flipped_sb[:, k, :], identity[:])
-            total_sq = sums[:, 1:N_SUMS, :].rearrange("p k j -> p (k j)")
-
-            mean_sq = work.tile([P, CHUNK], F32, name="mean_sq")
-            for first, total in ((0, sums[:, 0, :]), (HALF, second_total[:])):
-                nc.scalar.activation(
-                    cat[:, 1, i * CHUNK + first : i * CHUNK + first + HALF], total, ACT.Copy, scale=1.0 / MSGS
-                )
-                nc.scalar.activation(mean_sq[:, first : first + HALF], total, ACT.Square, scale=1.0 / MSGS)
-            var = work.tile([P, CHUNK], F32, name="var")
-            nc.vector.scalar_tensor_tensor(var[:], total_sq, 1.0 / MSGS, mean_sq[:], ALU.mult, ALU.subtract)
-            nc.vector.tensor_scalar(var[:], var[:], 0.0, EPS, ALU.max, ALU.add)
-            nc.scalar.activation(cat[:, 4, nodes], var[:], ACT.Sqrt)
-
             h_ps = psum_h.tile([P, CHUNK], F32, name="h_ps")
-            for b in range(BLOCKS):
-                nc.tensor.matmul(h_ps[:], w_post_sb[:, b, :], cat[:, b, nodes], start=(b == 0), stop=(b == BLOCKS - 1))
+            order = (0, 1, 4, 2, 3)
+            for b in order:
+                nc.tensor.matmul(h_ps[:], w_post_sb[:, b, :], cat[:, b, nodes], start=(b == order[0]), stop=(b == order[-1]))
             h_bf = work.tile([P, CHUNK], BF16, name="h_bf")
             nc.scalar.copy(h_bf[:], h_ps[:])
             u_chunk = u_banks[i * CHUNK // BANK][:, (i * CHUNK) % BANK : (i * CHUNK) % BANK + CHUNK]
             nc.tensor.matmul(u_chunk, w_lin_sb[:], h_bf[:], start=True, stop=True)
             nc.vector.bn_stats(u_stats[:, i, :], u_chunk)
 
-        partial = aggregate(0)
-        for i in range(1, N_CHUNKS):
-            earlier = partial
-            partial = aggregate(i)
-            finish(i - 1, earlier[0], earlier[1])
-        finish(N_CHUNKS - 1, partial[0], partial[1])
+        ahead = sums(0)
+        for i in range(N_CHUNKS):
+            flipped, vector_totals, second_bf = ahead
+            if i + 1 < N_CHUNKS:
+                ahead = sums(i + 1)
+            mean_and_std(i, flipped, vector_totals)
+            min_and_max(i, second_bf)
+            matmuls(i)
 
         mean_var = held.tile([P, 2], F32, name="mean_var")
         nc.vector.bn_aggr(mean_var[:], u_stats[:].rearrange("p c s -> p (c s)"))

@@ -41,20 +41,27 @@ def tile_gnnlayer_kernel(tc, base, x, m, w_post, w_lin, gn_w, gn_b, gn_alpha, of
         nc.sync.dma_start(offsets[:], offs)
         msg_tiles = [msgs.tile([P, CHUNK, MSGS], F32, name="msg") for i in range(N_CHUNKS)]
 
+        def pieces(i, k):
+            n_pieces = 4 if (i, k) == (0, 0) else 1
+            width = HALF // n_pieces
+            return [slice(k * HALF + q * width, k * HALF + (q + 1) * width) for q in range(n_pieces)]
+
         def load_messages(i):
-            for first in (0, HALF):
-                nc.sync.dma_start(
-                    msg_tiles[i][:, first : first + HALF, :], m[:, i * CHUNK + first : i * CHUNK + first + HALF, :]
-                )
+            for k in range(2):
+                for piece in pieces(i, k):
+                    nc.sync.dma_start(
+                        msg_tiles[i][:, piece, :], m[:, i * CHUNK + piece.start : i * CHUNK + piece.stop, :]
+                    )
 
         load_messages(0)
+        load_messages(1)
         w_post_sb = held.tile([P, BLOCKS, P], BF16, name="w_post_sb")
         nc.sync.dma_start(w_post_sb[:], w_post.rearrange("(b r) d -> r b d", r=P))
         w_lin_sb = held.tile([P, P], BF16, name="w_lin_sb")
         nc.sync.dma_start(w_lin_sb[:], w_lin)
         x_f32 = held.tile([P, NODES], F32, name="x_f32")
         nc.sync.dma_start(x_f32[:], x)
-        for i in range(1, N_CHUNKS):
+        for i in range(2, N_CHUNKS):
             load_messages(i)
         weight = held.tile([P, 1], F32, name="weight")
         nc.sync.dma_start(weight[:], gn_w)
@@ -86,7 +93,7 @@ def tile_gnnlayer_kernel(tc, base, x, m, w_post, w_lin, gn_w, gn_b, gn_alpha, of
                 )
 
         def tensor_engine_sums_messages(i, k):
-            return k == 0 and i < N_CHUNKS - 1
+            return k == 0 and i > 0
 
         def sums(i):
             halves = (slice(0, HALF), slice(HALF, CHUNK))
@@ -97,9 +104,11 @@ def tile_gnnlayer_kernel(tc, base, x, m, w_post, w_lin, gn_w, gn_b, gn_alpha, of
                 if tensor_engine_sums_messages(i, k):
                     sum_flipped(flipped[:, 2, :], msg_tiles[i][:, half, :])
                 else:
-                    nc.vector.tensor_reduce(vector_totals[:, half], msg_tiles[i][:, half, :], X_AXIS, ALU.add)
+                    for piece in pieces(i, k):
+                        nc.vector.tensor_reduce(vector_totals[:, piece], msg_tiles[i][:, piece, :], X_AXIS, ALU.add)
             for k, half in enumerate(halves):
-                nc.scalar.activation(squares[:, half, :], msg_tiles[i][:, half, :], ACT.Square)
+                for piece in pieces(i, k):
+                    nc.scalar.activation(squares[:, piece, :], msg_tiles[i][:, piece, :], ACT.Square)
                 sum_flipped(flipped[:, k, :], squares[:, half, :])
             second_bf = copies.tile([P, HALF, MSGS], BF16, name="second_bf")
             nc.scalar.copy(second_bf[:], msg_tiles[i][:, HALF:CHUNK, :])
@@ -132,11 +141,13 @@ def tile_gnnlayer_kernel(tc, base, x, m, w_post, w_lin, gn_w, gn_b, gn_alpha, of
 
         def min_and_max(i, second_bf):
             nodes = slice(i * CHUNK, (i + 1) * CHUNK)
-            first_half = msg_tiles[i][:, 0:HALF, :]
             for block, op, label in ((2, ALU.min, "min"), (3, ALU.max, "max")):
                 width = MSGS // 2
                 folded = folds.tile([P, CHUNK, width], BF16, name=f"{label}{width}")
-                nc.vector.tensor_tensor(folded[:, 0:HALF, :], first_half[:, :, 0:width], first_half[:, :, width:MSGS], op)
+                for piece in pieces(i, 0):
+                    nc.vector.tensor_tensor(
+                        folded[:, piece, :], msg_tiles[i][:, piece, 0:width], msg_tiles[i][:, piece, width:MSGS], op
+                    )
                 nc.vector.tensor_tensor(folded[:, HALF:CHUNK, :], second_bf[:, :, 0:width], second_bf[:, :, width:MSGS], op)
                 while width > 2:
                     width //= 2

@@ -95,6 +95,9 @@ def tile_gnnlayer_kernel(tc, base, x, m, w_post, w_lin, gn_w, gn_b, gn_alpha, of
         def tensor_engine_sums_messages(i, k):
             return k == 0 and i > 0
 
+        def copied(i, k):
+            return k == 1 or i > 0
+
         def sums(i):
             halves = (slice(0, HALF), slice(HALF, CHUNK))
             flipped = psum_flipped.tile([P, N_SUMS, HALF], F32, name="flipped")
@@ -110,9 +113,11 @@ def tile_gnnlayer_kernel(tc, base, x, m, w_post, w_lin, gn_w, gn_b, gn_alpha, of
                 for piece in pieces(i, k):
                     nc.scalar.activation(squares[:, piece, :], msg_tiles[i][:, piece, :], ACT.Square)
                 sum_flipped(flipped[:, k, :], squares[:, half, :])
-            second_bf = copies.tile([P, HALF, MSGS], BF16, name="second_bf")
-            nc.scalar.copy(second_bf[:], msg_tiles[i][:, HALF:CHUNK, :])
-            return flipped, vector_totals, second_bf
+            msgs_bf = copies.tile([P, CHUNK, MSGS], BF16, name="msgs_bf")
+            nc.scalar.copy(msgs_bf[:, HALF:CHUNK, :], msg_tiles[i][:, HALF:CHUNK, :])
+            if copied(i, 0):
+                nc.gpsimd.tensor_copy(msgs_bf[:, 0:HALF, :], msg_tiles[i][:, 0:HALF, :])
+            return flipped, vector_totals, msgs_bf
 
         def mean_and_std(i, flipped, vector_totals):
             nodes = slice(i * CHUNK, (i + 1) * CHUNK)
@@ -120,7 +125,7 @@ def tile_gnnlayer_kernel(tc, base, x, m, w_post, w_lin, gn_w, gn_b, gn_alpha, of
             flipped_sb = work.tile([P, N_SUMS, HALF], F32, name="flipped_sb")
             nc.scalar.copy(flipped_sb[:, 0:n_flipped, :], flipped[:, 0:n_flipped, :])
             sums_ps = psum_sums.tile([P, N_SUMS, HALF], F32, name="sums_ps")
-            for k in range(n_flipped):
+            for k in reversed(range(n_flipped)):
                 nc.tensor.transpose(sums_ps[:, k, :], flipped_sb[:, k, :], identity[:])
             total_sq = sums_ps[:, 0:2, :].rearrange("p k j -> p (k j)")
 
@@ -130,25 +135,27 @@ def tile_gnnlayer_kernel(tc, base, x, m, w_post, w_lin, gn_w, gn_b, gn_alpha, of
             else:
                 pieces = ((slice(0, CHUNK), vector_totals[:]),)
             for piece, total in pieces:
-                nc.scalar.activation(
-                    cat[:, 1, i * CHUNK + piece.start : i * CHUNK + piece.stop], total, ACT.Copy, scale=1.0 / MSGS
-                )
                 nc.scalar.activation(mean_sq[:, piece], total, ACT.Square, scale=1.0 / MSGS)
             var = work.tile([P, CHUNK], F32, name="var")
             nc.vector.scalar_tensor_tensor(var[:], total_sq, 1.0 / MSGS, mean_sq[:], ALU.mult, ALU.subtract)
             nc.vector.tensor_scalar(var[:], var[:], 0.0, EPS, ALU.max, ALU.add)
+            for piece, total in pieces:
+                nc.scalar.activation(
+                    cat[:, 1, i * CHUNK + piece.start : i * CHUNK + piece.stop], total, ACT.Copy, scale=1.0 / MSGS
+                )
             nc.scalar.activation(cat[:, 4, nodes], var[:], ACT.Sqrt)
 
-        def min_and_max(i, second_bf):
+        def min_and_max(i, msgs_bf):
             nodes = slice(i * CHUNK, (i + 1) * CHUNK)
             for block, op, label in ((2, ALU.min, "min"), (3, ALU.max, "max")):
                 width = MSGS // 2
                 folded = folds.tile([P, CHUNK, width], BF16, name=f"{label}{width}")
-                for piece in pieces(i, 0):
-                    nc.vector.tensor_tensor(
-                        folded[:, piece, :], msg_tiles[i][:, piece, 0:width], msg_tiles[i][:, piece, width:MSGS], op
-                    )
-                nc.vector.tensor_tensor(folded[:, HALF:CHUNK, :], second_bf[:, :, 0:width], second_bf[:, :, width:MSGS], op)
+                for k in range(2):
+                    source = msgs_bf if copied(i, k) else msg_tiles[i]
+                    for piece in pieces(i, k):
+                        nc.vector.tensor_tensor(
+                            folded[:, piece, :], source[:, piece, 0:width], source[:, piece, width:MSGS], op
+                        )
                 while width > 2:
                     width //= 2
                     halved = folds.tile([P, CHUNK, width], BF16, name=f"{label}{width}")
@@ -170,11 +177,11 @@ def tile_gnnlayer_kernel(tc, base, x, m, w_post, w_lin, gn_w, gn_b, gn_alpha, of
 
         ahead = sums(0)
         for i in range(N_CHUNKS):
-            flipped, vector_totals, second_bf = ahead
+            flipped, vector_totals, msgs_bf = ahead
             if i + 1 < N_CHUNKS:
                 ahead = sums(i + 1)
             mean_and_std(i, flipped, vector_totals)
-            min_and_max(i, second_bf)
+            min_and_max(i, msgs_bf)
             matmuls(i)
 
         mean_var = held.tile([P, 2], F32, name="mean_var")

@@ -93,7 +93,7 @@ def tile_gnnlayer_kernel(tc, base, x, m, w_post, w_lin, gn_w, gn_b, gn_alpha, of
                 )
 
         def tensor_engine_sums_messages(i, k):
-            return k == 0 and i > 0
+            return k == 0 and 0 < i < N_CHUNKS - 1
 
         def copied(i, k):
             return k == 1 or i > 0

@@ -16,7 +16,7 @@ BLOCKS = 5
 HALF = 128
 CHUNK = 2 * HALF
 N_CHUNKS = NODES // CHUNK
-N_SUMS = 3
+N_SUMS = 4
 BANK = 512
 BN_STATS = 6
 EPS = 1e-5
@@ -93,10 +93,16 @@ def tile_gnnlayer_kernel(tc, base, x, m, w_post, w_lin, gn_w, gn_b, gn_alpha, of
                 )
 
         def tensor_engine_sums_messages(i, k):
-            return k == 0 and 0 < i < N_CHUNKS - 1
+            return 0 < i < N_CHUNKS - 1
 
         def copied(i, k):
-            return k == 1 or i > 0
+            return gpsimd_copies(i, k) or scalar_copies(i, k)
+
+        def gpsimd_copies(i, k):
+            return i % 2 == 1 and k == 0
+
+        def scalar_copies(i, k):
+            return i >= N_CHUNKS // 2 and k == 1
 
         def sums(i):
             halves = (slice(0, HALF), slice(HALF, CHUNK))
@@ -105,7 +111,7 @@ def tile_gnnlayer_kernel(tc, base, x, m, w_post, w_lin, gn_w, gn_b, gn_alpha, of
             vector_totals = work.tile([P, CHUNK], F32, name="vector_totals")
             for k, half in enumerate(halves):
                 if tensor_engine_sums_messages(i, k):
-                    sum_flipped(flipped[:, 2, :], msg_tiles[i][:, half, :])
+                    sum_flipped(flipped[:, 2 + k, :], msg_tiles[i][:, half, :])
                 else:
                     for piece in pieces(i, k):
                         nc.vector.tensor_reduce(vector_totals[:, piece], msg_tiles[i][:, piece, :], X_AXIS, ALU.add)
@@ -113,15 +119,11 @@ def tile_gnnlayer_kernel(tc, base, x, m, w_post, w_lin, gn_w, gn_b, gn_alpha, of
                 for piece in pieces(i, k):
                     nc.scalar.activation(squares[:, piece, :], msg_tiles[i][:, piece, :], ACT.Square)
                 sum_flipped(flipped[:, k, :], squares[:, half, :])
-            msgs_bf = copies.tile([P, CHUNK, MSGS], BF16, name="msgs_bf")
-            nc.scalar.copy(msgs_bf[:, HALF:CHUNK, :], msg_tiles[i][:, HALF:CHUNK, :])
-            if copied(i, 0):
-                nc.gpsimd.tensor_copy(msgs_bf[:, 0:HALF, :], msg_tiles[i][:, 0:HALF, :])
-            return flipped, vector_totals, msgs_bf
+            return flipped, vector_totals
 
         def mean_and_std(i, flipped, vector_totals):
             nodes = slice(i * CHUNK, (i + 1) * CHUNK)
-            n_flipped = 3 if tensor_engine_sums_messages(i, 0) else 2
+            n_flipped = 2 + sum(tensor_engine_sums_messages(i, k) for k in range(2))
             flipped_sb = work.tile([P, N_SUMS, HALF], F32, name="flipped_sb")
             nc.scalar.copy(flipped_sb[:, 0:n_flipped, :], flipped[:, 0:n_flipped, :])
             sums_ps = psum_sums.tile([P, N_SUMS, HALF], F32, name="sums_ps")
@@ -130,7 +132,9 @@ def tile_gnnlayer_kernel(tc, base, x, m, w_post, w_lin, gn_w, gn_b, gn_alpha, of
             total_sq = sums_ps[:, 0:2, :].rearrange("p k j -> p (k j)")
 
             mean_sq = work.tile([P, CHUNK], F32, name="mean_sq")
-            if tensor_engine_sums_messages(i, 0):
+            if n_flipped == 4:
+                pieces = ((slice(0, CHUNK), sums_ps[:, 2:4, :].rearrange("p k j -> p (k j)")),)
+            elif n_flipped == 3:
                 pieces = ((slice(0, HALF), sums_ps[:, 2, :]), (slice(HALF, CHUNK), vector_totals[:, HALF:CHUNK]))
             else:
                 pieces = ((slice(0, CHUNK), vector_totals[:]),)
@@ -144,6 +148,15 @@ def tile_gnnlayer_kernel(tc, base, x, m, w_post, w_lin, gn_w, gn_b, gn_alpha, of
                     cat[:, 1, i * CHUNK + piece.start : i * CHUNK + piece.stop], total, ACT.Copy, scale=1.0 / MSGS
                 )
             nc.scalar.activation(cat[:, 4, nodes], var[:], ACT.Sqrt)
+
+        def make_copies(i):
+            msgs_bf = copies.tile([P, CHUNK, MSGS], BF16, name="msgs_bf") if i > 0 else None
+            for k, half in enumerate((slice(0, HALF), slice(HALF, CHUNK))):
+                if gpsimd_copies(i, k):
+                    nc.gpsimd.tensor_copy(msgs_bf[:, half, :], msg_tiles[i][:, half, :])
+                elif scalar_copies(i, k):
+                    nc.scalar.copy(msgs_bf[:, half, :], msg_tiles[i][:, half, :])
+            return msgs_bf
 
         def min_and_max(i, msgs_bf):
             nodes = slice(i * CHUNK, (i + 1) * CHUNK)
@@ -163,7 +176,7 @@ def tile_gnnlayer_kernel(tc, base, x, m, w_post, w_lin, gn_w, gn_b, gn_alpha, of
                     folded = halved
                 nc.vector.tensor_tensor(cat[:, block, nodes], folded[:, :, 0], folded[:, :, 1], op)
 
-        def matmuls(i):
+        def hidden(i):
             nodes = slice(i * CHUNK, (i + 1) * CHUNK)
             h_ps = psum_h.tile([P, CHUNK], F32, name="h_ps")
             order = (0, 1, 4, 2, 3)
@@ -171,18 +184,28 @@ def tile_gnnlayer_kernel(tc, base, x, m, w_post, w_lin, gn_w, gn_b, gn_alpha, of
                 nc.tensor.matmul(h_ps[:], w_post_sb[:, b, :], cat[:, b, nodes], start=(b == order[0]), stop=(b == order[-1]))
             h_bf = work.tile([P, CHUNK], BF16, name="h_bf")
             nc.scalar.copy(h_bf[:], h_ps[:])
+            return h_bf
+
+        def update(i, h_bf):
             u_chunk = u_banks[i * CHUNK // BANK][:, (i * CHUNK) % BANK : (i * CHUNK) % BANK + CHUNK]
             nc.tensor.matmul(u_chunk, w_lin_sb[:], h_bf[:], start=True, stop=True)
             nc.vector.bn_stats(u_stats[:, i, :], u_chunk)
 
         ahead = sums(0)
+        h_chunks = []
         for i in range(N_CHUNKS):
-            flipped, vector_totals, msgs_bf = ahead
+            flipped, vector_totals = ahead
             if i + 1 < N_CHUNKS:
                 ahead = sums(i + 1)
             mean_and_std(i, flipped, vector_totals)
-            min_and_max(i, msgs_bf)
-            matmuls(i)
+            if i > 0:
+                h_chunks.append(hidden(i - 1))
+            if i > 1:
+                update(i - 2, h_chunks[i - 2])
+            min_and_max(i, make_copies(i))
+        h_chunks.append(hidden(N_CHUNKS - 1))
+        for i in range(N_CHUNKS - 2, N_CHUNKS):
+            update(i, h_chunks[i])
 
         mean_var = held.tile([P, 2], F32, name="mean_var")
         nc.vector.bn_aggr(mean_var[:], u_stats[:].rearrange("p c s -> p (c s)"))

@@ -75,6 +75,11 @@ def tile_gnnlayer_kernel(tc, base, x, m, w_post, w_lin, gn_w, gn_b, gn_alpha, of
         identity = held.tile([P, P], F32, name="identity")
         make_identity(nc, identity[:])
 
+        ones = held.tile([P, 1], F32, name="ones")
+        nc.vector.memset(ones[:], 1.0)
+        root = held.tile([P, 1], F32, name="root")
+        nc.scalar.activation(root[:], ones[:], ACT.Sqrt)
+
         cat = held.tile([P, BLOCKS, NODES], BF16, name="cat")
         nc.vector.tensor_copy(cat[:, 0, :], x_f32[:])
 

@@ -17,7 +17,6 @@ HALF = 128
 CHUNK = 2 * HALF
 N_CHUNKS = NODES // CHUNK
 N_SUMS = 4
-BANK = 512
 BN_STATS = 6
 EPS = 1e-5
 
@@ -34,8 +33,7 @@ def tile_gnnlayer_kernel(tc, base, x, m, w_post, w_lin, gn_w, gn_b, gn_alpha, of
         tc.tile_pool(name="work", bufs=3) as work,
         tc.psum_pool(name="psum_flipped", bufs=2) as psum_flipped,
         tc.psum_pool(name="psum_sums", bufs=2) as psum_sums,
-        tc.psum_pool(name="psum_h", bufs=2) as psum_h,
-        tc.psum_pool(name="psum_u", bufs=1) as psum_u,
+        tc.psum_pool(name="psum_hu", bufs=1) as psum_hu,
     ):
         offsets = held.tile([P, NODES // 16], U16, name="offsets")
         nc.sync.dma_start(offsets[:], offs)
@@ -88,7 +86,9 @@ def tile_gnnlayer_kernel(tc, base, x, m, w_post, w_lin, gn_w, gn_b, gn_alpha, of
         minus_w_alpha = held.tile([P, 1], F32, name="minus_w_alpha")
         nc.vector.scalar_tensor_tensor(minus_w_alpha[:], weight[:], -1.0, alpha[:], ALU.mult, ALU.mult)
 
-        u_banks = [psum_u.tile([P, BANK], F32, name=f"u_bank{k}") for k in range(NODES // BANK)]
+        hu_banks = [psum_hu.tile([P, 2, CHUNK], F32, name=f"hu{i}") for i in range(N_CHUNKS)]
+        h_chunks = [bank[:, 0, :] for bank in hu_banks]
+        u_chunks = [bank[:, 1, :] for bank in hu_banks]
         u_stats = held.tile([P, N_CHUNKS, BN_STATS], F32, name="u_stats")
 
         def sum_flipped(flipped_sum, values):
@@ -98,16 +98,10 @@ def tile_gnnlayer_kernel(tc, base, x, m, w_post, w_lin, gn_w, gn_b, gn_alpha, of
                 )
 
         def tensor_engine_sums_messages(i, k):
-            return 0 < i < N_CHUNKS - 1
+            return 2 <= 2 * i + k <= 4
 
         def copied(i, k):
-            return gpsimd_copies(i, k) or scalar_copies(i, k)
-
-        def gpsimd_copies(i, k):
-            return i % 2 == 1 and k == 0
-
-        def scalar_copies(i, k):
-            return i >= N_CHUNKS // 2 and k == 1
+            return (i > 0 and k == 0) or (i, k) == (2, 1)
 
         def sums(i):
             halves = (slice(0, HALF), slice(HALF, CHUNK))
@@ -124,7 +118,11 @@ def tile_gnnlayer_kernel(tc, base, x, m, w_post, w_lin, gn_w, gn_b, gn_alpha, of
                 for piece in pieces(i, k):
                     nc.scalar.activation(squares[:, piece, :], msg_tiles[i][:, piece, :], ACT.Square)
                 sum_flipped(flipped[:, k, :], squares[:, half, :])
-            return flipped, vector_totals
+            msgs_bf = copies.tile([P, CHUNK, MSGS], BF16, name="msgs_bf") if copied(i, 0) else None
+            for k, half in enumerate(halves):
+                if copied(i, k):
+                    nc.scalar.copy(msgs_bf[:, half, :], msg_tiles[i][:, half, :])
+            return flipped, vector_totals, msgs_bf
 
         def mean_and_std(i, flipped, vector_totals):
             nodes = slice(i * CHUNK, (i + 1) * CHUNK)
@@ -154,15 +152,6 @@ def tile_gnnlayer_kernel(tc, base, x, m, w_post, w_lin, gn_w, gn_b, gn_alpha, of
                 )
             nc.scalar.activation(cat[:, 4, nodes], var[:], ACT.Sqrt)
 
-        def make_copies(i):
-            msgs_bf = copies.tile([P, CHUNK, MSGS], BF16, name="msgs_bf") if i > 0 else None
-            for k, half in enumerate((slice(0, HALF), slice(HALF, CHUNK))):
-                if gpsimd_copies(i, k):
-                    nc.gpsimd.tensor_copy(msgs_bf[:, half, :], msg_tiles[i][:, half, :])
-                elif scalar_copies(i, k):
-                    nc.scalar.copy(msgs_bf[:, half, :], msg_tiles[i][:, half, :])
-            return msgs_bf
-
         def min_and_max(i, msgs_bf):
             nodes = slice(i * CHUNK, (i + 1) * CHUNK)
             for block, op, label in ((2, ALU.min, "min"), (3, ALU.max, "max")):
@@ -183,34 +172,32 @@ def tile_gnnlayer_kernel(tc, base, x, m, w_post, w_lin, gn_w, gn_b, gn_alpha, of
 
         def hidden(i):
             nodes = slice(i * CHUNK, (i + 1) * CHUNK)
-            h_ps = psum_h.tile([P, CHUNK], F32, name="h_ps")
             order = (0, 1, 4, 2, 3)
             for b in order:
-                nc.tensor.matmul(h_ps[:], w_post_sb[:, b, :], cat[:, b, nodes], start=(b == order[0]), stop=(b == order[-1]))
+                nc.tensor.matmul(h_chunks[i], w_post_sb[:, b, :], cat[:, b, nodes], start=(b == order[0]), stop=(b == order[-1]))
             h_bf = work.tile([P, CHUNK], BF16, name="h_bf")
-            nc.scalar.copy(h_bf[:], h_ps[:])
+            nc.scalar.copy(h_bf[:], h_chunks[i])
             return h_bf
 
         def update(i, h_bf):
-            u_chunk = u_banks[i * CHUNK // BANK][:, (i * CHUNK) % BANK : (i * CHUNK) % BANK + CHUNK]
-            nc.tensor.matmul(u_chunk, w_lin_sb[:], h_bf[:], start=True, stop=True)
-            nc.vector.bn_stats(u_stats[:, i, :], u_chunk)
+            nc.tensor.matmul(u_chunks[i], w_lin_sb[:], h_bf[:], start=True, stop=True)
+            nc.vector.bn_stats(u_stats[:, i, :], u_chunks[i])
 
         ahead = sums(0)
-        h_chunks = []
+        hs = []
         for i in range(N_CHUNKS):
-            flipped, vector_totals = ahead
+            flipped, vector_totals, msgs_bf = ahead
             if i + 1 < N_CHUNKS:
                 ahead = sums(i + 1)
             mean_and_std(i, flipped, vector_totals)
             if i > 0:
-                h_chunks.append(hidden(i - 1))
+                hs.append(hidden(i - 1))
             if i > 1:
-                update(i - 2, h_chunks[i - 2])
-            min_and_max(i, make_copies(i))
-        h_chunks.append(hidden(N_CHUNKS - 1))
-        for i in range(N_CHUNKS - 2, N_CHUNKS):
-            update(i, h_chunks[i])
+                update(i - 2, hs[i - 2])
+            if i == N_CHUNKS - 1:
+                update(i - 1, hs[i - 1])
+            min_and_max(i, msgs_bf)
+        update(N_CHUNKS - 1, hidden(N_CHUNKS - 1))
 
         mean_var = held.tile([P, 2], F32, name="mean_var")
         nc.vector.bn_aggr(mean_var[:], u_stats[:].rearrange("p c s -> p (c s)"))
@@ -231,8 +218,13 @@ def tile_gnnlayer_kernel(tc, base, x, m, w_post, w_lin, gn_w, gn_b, gn_alpha, of
         offset = held.tile([P, 1], F32, name="offset")
         nc.vector.tensor_scalar(offset[:], inv_norm[:], minus_w_alpha_mu[:], shift[:], ALU.mult, ALU.add)
         y = held.tile([P, NODES], F32, name="y")
-        for k, u_bank in enumerate(u_banks):
-            nc.scalar.activation(y[:, k * BANK : (k + 1) * BANK], u_bank[:], ACT.Relu, bias=offset[:], scale=gain[:])
+        for i, u_chunk in enumerate(u_chunks):
+            nodes = slice(i * CHUNK, (i + 1) * CHUNK)
+            if i < N_CHUNKS - 1:
+                nc.scalar.activation(y[:, nodes], u_chunk, ACT.Relu, bias=offset[:], scale=gain[:])
+            else:
+                nc.vector.tensor_scalar(y[:, nodes], u_chunk, gain[:], offset[:], ALU.mult, ALU.add)
+                nc.vector.tensor_scalar_max(y[:, nodes], y[:, nodes], 0.0)
 
         nc.vector.tensor_tensor(store[:].indirect(offsets[:]), y[:], x_f32[:], ALU.add)
         nc.sync.dma_start(out, store[:])

@@ -101,7 +101,7 @@ def tile_gnnlayer_kernel(tc, base, x, m, w_post, w_lin, gn_w, gn_b, gn_alpha, of
             return 2 <= 2 * i + k <= 4
 
         def copied(i, k):
-            return (i > 0 and k == 0) or (i, k) == (2, 1)
+            return (i > 0 and k == 0) or (i, k) == (N_CHUNKS - 1, 1)
 
         def sums(i):
             halves = (slice(0, HALF), slice(HALF, CHUNK))
@@ -118,11 +118,7 @@ def tile_gnnlayer_kernel(tc, base, x, m, w_post, w_lin, gn_w, gn_b, gn_alpha, of
                 for piece in pieces(i, k):
                     nc.scalar.activation(squares[:, piece, :], msg_tiles[i][:, piece, :], ACT.Square)
                 sum_flipped(flipped[:, k, :], squares[:, half, :])
-            msgs_bf = copies.tile([P, CHUNK, MSGS], BF16, name="msgs_bf") if copied(i, 0) else None
-            for k, half in enumerate(halves):
-                if copied(i, k):
-                    nc.scalar.copy(msgs_bf[:, half, :], msg_tiles[i][:, half, :])
-            return flipped, vector_totals, msgs_bf
+            return flipped, vector_totals
 
         def mean_and_std(i, flipped, vector_totals):
             nodes = slice(i * CHUNK, (i + 1) * CHUNK)
@@ -151,6 +147,13 @@ def tile_gnnlayer_kernel(tc, base, x, m, w_post, w_lin, gn_w, gn_b, gn_alpha, of
                     cat[:, 1, i * CHUNK + piece.start : i * CHUNK + piece.stop], total, ACT.Copy, scale=1.0 / MSGS
                 )
             nc.scalar.activation(cat[:, 4, nodes], var[:], ACT.Sqrt)
+
+        def copy_messages(i):
+            msgs_bf = copies.tile([P, CHUNK, MSGS], BF16, name="msgs_bf") if copied(i, 0) else None
+            for k, half in enumerate((slice(0, HALF), slice(HALF, CHUNK))):
+                if copied(i, k):
+                    nc.scalar.copy(msgs_bf[:, half, :], msg_tiles[i][:, half, :])
+            return msgs_bf
 
         def min_and_max(i, msgs_bf):
             nodes = slice(i * CHUNK, (i + 1) * CHUNK)
@@ -186,7 +189,7 @@ def tile_gnnlayer_kernel(tc, base, x, m, w_post, w_lin, gn_w, gn_b, gn_alpha, of
         ahead = sums(0)
         hs = []
         for i in range(N_CHUNKS):
-            flipped, vector_totals, msgs_bf = ahead
+            flipped, vector_totals = ahead
             if i + 1 < N_CHUNKS:
                 ahead = sums(i + 1)
             mean_and_std(i, flipped, vector_totals)
@@ -196,7 +199,7 @@ def tile_gnnlayer_kernel(tc, base, x, m, w_post, w_lin, gn_w, gn_b, gn_alpha, of
                 update(i - 2, hs[i - 2])
             if i == N_CHUNKS - 1:
                 update(i - 1, hs[i - 1])
-            min_and_max(i, msgs_bf)
+            min_and_max(i, copy_messages(i))
         update(N_CHUNKS - 1, hidden(N_CHUNKS - 1))
 
         mean_var = held.tile([P, 2], F32, name="mean_var")

@@ -79,7 +79,6 @@ def tile_gnnlayer_kernel(tc, base, x, m, w_post, w_lin, gn_w, gn_b, gn_alpha, of
         nc.scalar.activation(root[:], ones[:], ACT.Sqrt)
 
         cat = held.tile([P, BLOCKS, NODES], BF16, name="cat")
-        nc.vector.tensor_copy(cat[:, 0, :], x_f32[:])
 
         one_minus_alpha = held.tile([P, 1], F32, name="one_minus_alpha")
         nc.vector.tensor_scalar(one_minus_alpha[:], alpha[:], -1.0, 1.0, ALU.mult, ALU.add)
@@ -175,6 +174,7 @@ def tile_gnnlayer_kernel(tc, base, x, m, w_post, w_lin, gn_w, gn_b, gn_alpha, of
 
         def hidden(i):
             nodes = slice(i * CHUNK, (i + 1) * CHUNK)
+            nc.scalar.copy(cat[:, 0, nodes], x_f32[:, nodes])
             order = (0, 1, 4, 2, 3)
             for b in order:
                 nc.tensor.matmul(h_chunks[i], w_post_sb[:, b, :], cat[:, b, nodes], start=(b == order[0]), stop=(b == order[-1]))

@@ -40,7 +40,7 @@ def tile_gnnlayer_kernel(tc, base, x, m, w_post, w_lin, gn_w, gn_b, gn_alpha, of
         msg_tiles = [msgs.tile([P, CHUNK, MSGS], F32, name="msg") for i in range(N_CHUNKS)]
 
         def pieces(i, k):
-            n_pieces = 4 if (i, k) == (0, 0) else 1
+            n_pieces = 4 if i == 0 else 1
             width = HALF // n_pieces
             return [slice(k * HALF + q * width, k * HALF + (q + 1) * width) for q in range(n_pieces)]
 

import concourse.mybir as mybir
from concourse.masks import make_identity

F32 = mybir.dt.float32
BF16 = mybir.dt.bfloat16
U16 = mybir.dt.uint16
ALU = mybir.AluOpType
ACT = mybir.ActivationFunctionType
X_AXIS = mybir.AxisListType.X

P = 128
STORE = 2048
NODES = 1024
MSGS = 16
BLOCKS = 5
HALF = 128
CHUNK = 2 * HALF
N_CHUNKS = NODES // CHUNK
N_SUMS = 4
BN_STATS = 6
EPS = 1e-5

FLOPS = 2 * BLOCKS * P * P * NODES + 2 * P * P * NODES


def tile_gnnlayer_kernel(tc, base, x, m, w_post, w_lin, gn_w, gn_b, gn_alpha, offs, out):
    nc = tc.nc
    with (
        tc.tile_pool(name="held", bufs=1) as held,
        tc.tile_pool(name="msgs", bufs=N_CHUNKS) as msgs,
        tc.tile_pool(name="copies", bufs=2) as copies,
        tc.tile_pool(name="folds", bufs=2) as folds,
        tc.tile_pool(name="work", bufs=3) as work,
        tc.psum_pool(name="psum_flipped", bufs=2) as psum_flipped,
        tc.psum_pool(name="psum_sums", bufs=2) as psum_sums,
        tc.psum_pool(name="psum_hu", bufs=1) as psum_hu,
    ):
        offsets = held.tile([P, NODES // 16], U16, name="offsets")
        nc.sync.dma_start(offsets[:], offs)
        msg_tiles = [msgs.tile([P, CHUNK, MSGS], F32, name="msg") for i in range(N_CHUNKS)]

        def pieces(i, k):
            n_pieces = 4 if i == 0 else 1
            width = HALF // n_pieces
            return [slice(k * HALF + q * width, k * HALF + (q + 1) * width) for q in range(n_pieces)]

        def load_messages(i):
            for k in range(2):
                for piece in pieces(i, k):
                    nc.sync.dma_start(
                        msg_tiles[i][:, piece, :], m[:, i * CHUNK + piece.start : i * CHUNK + piece.stop, :]
                    )

        load_messages(0)
        load_messages(1)
        w_post_sb = held.tile([P, BLOCKS, P], BF16, name="w_post_sb")
        nc.sync.dma_start(w_post_sb[:], w_post.rearrange("(b r) d -> r b d", r=P))
        w_lin_sb = held.tile([P, P], BF16, name="w_lin_sb")
        nc.sync.dma_start(w_lin_sb[:], w_lin)
        x_f32 = held.tile([P, NODES], F32, name="x_f32")
        nc.sync.dma_start(x_f32[:], x)
        for i in range(2, N_CHUNKS):
            load_messages(i)
        weight = held.tile([P, 1], F32, name="weight")
        nc.sync.dma_start(weight[:], gn_w)
        shift = held.tile([P, 1], F32, name="shift")
        nc.sync.dma_start(shift[:], gn_b)
        alpha = held.tile([P, 1], F32, name="alpha")
        nc.sync.dma_start(alpha[:], gn_alpha)
        store = held.tile([P, STORE], F32, name="store")
        nc.sync.dma_start(store[:], base)

        identity = held.tile([P, P], F32, name="identity")
        make_identity(nc, identity[:])

        ones = held.tile([P, 1], F32, name="ones")
        nc.vector.memset(ones[:], 1.0)
        root = held.tile([P, 1], F32, name="root")
        nc.scalar.activation(root[:], ones[:], ACT.Sqrt)

        cat = held.tile([P, BLOCKS, NODES], BF16, name="cat")

        one_minus_alpha = held.tile([P, 1], F32, name="one_minus_alpha")
        nc.vector.tensor_scalar(one_minus_alpha[:], alpha[:], -1.0, 1.0, ALU.mult, ALU.add)
        minus_w_alpha = held.tile([P, 1], F32, name="minus_w_alpha")
        nc.vector.scalar_tensor_tensor(minus_w_alpha[:], weight[:], -1.0, alpha[:], ALU.mult, ALU.mult)

        hu_banks = [psum_hu.tile([P, 2, CHUNK], F32, name=f"hu{i}") for i in range(N_CHUNKS)]
        h_chunks = [bank[:, 0, :] for bank in hu_banks]
        u_chunks = [bank[:, 1, :] for bank in hu_banks]
        u_stats = held.tile([P, N_CHUNKS, BN_STATS], F32, name="u_stats")

        def sum_flipped(flipped_sum, values):
            for t in range(MSGS):
                nc.tensor.matmul(
                    flipped_sum, values[:, :, t], identity[:], start=(t == 0), stop=(t == MSGS - 1), is_transpose=True
                )

        def tensor_engine_sums_messages(i, k):
            return 2 <= 2 * i + k <= 4

        def copied(i, k):
            return (i > 0 and k == 0) or (i, k) == (N_CHUNKS - 1, 1)

        def sums(i):
            halves = (slice(0, HALF), slice(HALF, CHUNK))
            flipped = psum_flipped.tile([P, N_SUMS, HALF], F32, name="flipped")
            squares = copies.tile([P, CHUNK, MSGS], F32, name="squares")
            vector_totals = work.tile([P, CHUNK], F32, name="vector_totals")
            for k, half in enumerate(halves):
                if tensor_engine_sums_messages(i, k):
                    sum_flipped(flipped[:, 2 + k, :], msg_tiles[i][:, half, :])
                else:
                    for piece in pieces(i, k):
                        nc.vector.tensor_reduce(vector_totals[:, piece], msg_tiles[i][:, piece, :], X_AXIS, ALU.add)
            for k, half in enumerate(halves):
                for piece in pieces(i, k):
                    nc.scalar.activation(squares[:, piece, :], msg_tiles[i][:, piece, :], ACT.Square)
                sum_flipped(flipped[:, k, :], squares[:, half, :])
            return flipped, vector_totals

        def mean_and_std(i, flipped, vector_totals):
            nodes = slice(i * CHUNK, (i + 1) * CHUNK)
            n_flipped = 2 + sum(tensor_engine_sums_messages(i, k) for k in range(2))
            flipped_sb = work.tile([P, N_SUMS, HALF], F32, name="flipped_sb")
            nc.scalar.copy(flipped_sb[:, 0:n_flipped, :], flipped[:, 0:n_flipped, :])
            sums_ps = psum_sums.tile([P, N_SUMS, HALF], F32, name="sums_ps")
            for k in reversed(range(n_flipped)):
                nc.tensor.transpose(sums_ps[:, k, :], flipped_sb[:, k, :], identity[:])
            total_sq = sums_ps[:, 0:2, :].rearrange("p k j -> p (k j)")

            mean_sq = work.tile([P, CHUNK], F32, name="mean_sq")
            if n_flipped == 4:
                pieces = ((slice(0, CHUNK), sums_ps[:, 2:4, :].rearrange("p k j -> p (k j)")),)
            elif n_flipped == 3:
                pieces = ((slice(0, HALF), sums_ps[:, 2, :]), (slice(HALF, CHUNK), vector_totals[:, HALF:CHUNK]))
            else:
                pieces = ((slice(0, CHUNK), vector_totals[:]),)
            for piece, total in pieces:
                nc.scalar.activation(mean_sq[:, piece], total, ACT.Square, scale=1.0 / MSGS)
            var = work.tile([P, CHUNK], F32, name="var")
            nc.vector.scalar_tensor_tensor(var[:], total_sq, 1.0 / MSGS, mean_sq[:], ALU.mult, ALU.subtract)
            nc.vector.tensor_scalar(var[:], var[:], 0.0, EPS, ALU.max, ALU.add)
            for piece, total in pieces:
                nc.scalar.activation(
                    cat[:, 1, i * CHUNK + piece.start : i * CHUNK + piece.stop], total, ACT.Copy, scale=1.0 / MSGS
                )
            nc.scalar.activation(cat[:, 4, nodes], var[:], ACT.Sqrt)

        def copy_messages(i):
            msgs_bf = copies.tile([P, CHUNK, MSGS], BF16, name="msgs_bf") if copied(i, 0) else None
            for k, half in enumerate((slice(0, HALF), slice(HALF, CHUNK))):
                if copied(i, k):
                    nc.scalar.copy(msgs_bf[:, half, :], msg_tiles[i][:, half, :])
            return msgs_bf

        def min_and_max(i, msgs_bf):
            nodes = slice(i * CHUNK, (i + 1) * CHUNK)
            for block, op, label in ((2, ALU.min, "min"), (3, ALU.max, "max")):
                width = MSGS // 2
                folded = folds.tile([P, CHUNK, width], BF16, name=f"{label}{width}")
                for k in range(2):
                    source = msgs_bf if copied(i, k) else msg_tiles[i]
                    for piece in pieces(i, k):
                        nc.vector.tensor_tensor(
                            folded[:, piece, :], source[:, piece, 0:width], source[:, piece, width:MSGS], op
                        )
                while width > 2:
                    width //= 2
                    halved = folds.tile([P, CHUNK, width], BF16, name=f"{label}{width}")
                    nc.vector.tensor_tensor(halved[:], folded[:, :, 0:width], folded[:, :, width : 2 * width], op)
                    folded = halved
                nc.vector.tensor_tensor(cat[:, block, nodes], folded[:, :, 0], folded[:, :, 1], op)

        def hidden(i):
            nodes = slice(i * CHUNK, (i + 1) * CHUNK)
            nc.scalar.copy(cat[:, 0, nodes], x_f32[:, nodes])
            order = (0, 1, 4, 2, 3)
            for b in order:
                nc.tensor.matmul(h_chunks[i], w_post_sb[:, b, :], cat[:, b, nodes], start=(b == order[0]), stop=(b == order[-1]))
            h_bf = work.tile([P, CHUNK], BF16, name="h_bf")
            nc.scalar.copy(h_bf[:], h_chunks[i])
            return h_bf

        def update(i, h_bf):
            nc.tensor.matmul(u_chunks[i], w_lin_sb[:], h_bf[:], start=True, stop=True)
            nc.vector.bn_stats(u_stats[:, i, :], u_chunks[i])

        ahead = sums(0)
        hs = []
        for i in range(N_CHUNKS):
            flipped, vector_totals = ahead
            if i + 1 < N_CHUNKS:
                ahead = sums(i + 1)
            mean_and_std(i, flipped, vector_totals)
            if i > 0:
                hs.append(hidden(i - 1))
            if i > 1:
                update(i - 2, hs[i - 2])
            if i == N_CHUNKS - 1:
                update(i - 1, hs[i - 1])
            min_and_max(i, copy_messages(i))
        update(N_CHUNKS - 1, hidden(N_CHUNKS - 1))

        mean_var = held.tile([P, 2], F32, name="mean_var")
        nc.vector.bn_aggr(mean_var[:], u_stats[:].rearrange("p c s -> p (c s)"))
        mu = mean_var[:, 0:1]
        var_u = mean_var[:, 1:2]
        z_mean_sq = held.tile([P, 1], F32, name="z_mean_sq")
        nc.scalar.activation(z_mean_sq[:], mu, ACT.Square, scale=one_minus_alpha[:])
        var_eps = held.tile([P, 1], F32, name="var_eps")
        nc.vector.tensor_scalar_add(var_eps[:], var_u, EPS)
        minus_w_alpha_mu = held.tile([P, 1], F32, name="minus_w_alpha_mu")
        nc.vector.tensor_mul(minus_w_alpha_mu[:], minus_w_alpha[:], mu)
        norm = held.tile([P, 1], F32, name="norm")
        nc.scalar.activation(norm[:], z_mean_sq[:], ACT.Sqrt, bias=var_eps[:])
        inv_norm = held.tile([P, 1], F32, name="inv_norm")
        nc.vector.reciprocal(inv_norm[:], norm[:])
        gain = held.tile([P, 1], F32, name="gain")
        nc.vector.tensor_mul(gain[:], weight[:], inv_norm[:])
        offset = held.tile([P, 1], F32, name="offset")
        nc.vector.tensor_scalar(offset[:], inv_norm[:], minus_w_alpha_mu[:], shift[:], ALU.mult, ALU.add)
        y = held.tile([P, NODES], F32, name="y")
        for i, u_chunk in enumerate(u_chunks):
            nodes = slice(i * CHUNK, (i + 1) * CHUNK)
            if i < N_CHUNKS - 1:
                nc.scalar.activation(y[:, nodes], u_chunk, ACT.Relu, bias=offset[:], scale=gain[:])
            else:
                nc.vector.tensor_scalar(y[:, nodes], u_chunk, gain[:], offset[:], ALU.mult, ALU.add)
                nc.vector.tensor_scalar_max(y[:, nodes], y[:, nodes], 0.0)

        nc.vector.tensor_tensor(store[:].indirect(offsets[:]), y[:], x_f32[:], ALU.add)
        nc.sync.dma_start(out, store[:])
